import numpy as np
import ml_dtypes


def mxq(x, axis, fmt="e4m3"):
    dtype, down = {"e4m3": (ml_dtypes.float8_e4m3fn, 7), "e5m2": (ml_dtypes.float8_e5m2, 14)}[fmt]
    v = np.moveaxis(np.asarray(x, np.float32).astype(ml_dtypes.bfloat16).astype(np.float64), axis, -1)
    blocks = v.reshape(v.shape[:-1] + (-1, 32))
    amax = np.abs(blocks).max(-1, keepdims=True)
    byte = np.maximum(np.where(amax > 0, np.frexp(amax)[1] - 1 + 127, 0) - down, 1)
    scale = np.exp2(byte - 127.0)
    codes = (blocks / scale).astype(np.float32).astype(dtype).astype(np.float64)
    return np.moveaxis((codes * scale).reshape(v.shape), -1, axis)


WIDE = False


def mx_kscale(k):
    if not WIDE:
        return np.ones(k)
    levels = np.array([18, -18])
    if k % 512:
        return np.exp2(np.random.permutation(np.resize(levels, k // 32))).repeat(32)
    a = np.empty((k // 512, 16))
    for p in range(k // 512):
        a[p, :8] = np.random.permutation(np.resize(levels, 8))
        for g in range(8):
            far = levels[np.abs(levels - a[p, g]) >= 10]
            a[p, g + 8] = far[np.random.randint(len(far))]
    return np.exp2(a.ravel()).repeat(32)


BF16 = ml_dtypes.bfloat16


def bf(x):
    return np.asarray(x, np.float32).astype(BF16)


def f64(x):
    return np.asarray(x).astype(np.float64)


B, DIN, F, NCLS, NV = 1024, 1024, 1024, 18, 3
NJ = (F + NV - 1) // NV
S_NM = 2.0 / np.sqrt(DIN)
S_AN = 0.25 * np.sqrt(F / DIN)


def draw_view():
    x = bf(np.random.standard_normal((B, DIN)))
    w_nm = bf(np.random.standard_normal((DIN, F)) * S_NM)
    w_an = bf(np.random.standard_normal((DIN, F)) * S_AN)
    return x, w_nm, w_an


def setup_inputs():
    s = mx_kscale(B)[:, None]
    u = np.repeat(mx_kscale(F)[::96], 96)[:F]
    ug = np.concatenate([u[::NV], np.ones(F - NJ)])
    x0, wn0, wa0 = draw_view()
    x_rear, Wr_nm, Wr_an = draw_view()
    x_right, Wt_nm, Wt_an = draw_view()
    g = bf(np.random.standard_normal((B, F)) * np.exp2(np.random.randint(-6, 1, (B, 1))) * 4.0 / s * ug)
    nm = f64(x0) @ f64(wn0)
    gate = np.mean(f64(x0) @ f64(wa0), axis=1, keepdims=True)
    return {"x_dash": bf(f64(x0) * s), "x_rear": x_rear, "x_right": x_right,
            "Wd_nm": bf(f64(wn0) / u), "Wd_an": bf(f64(wa0) / np.max(u)),
            "Wr_nm": Wr_nm, "Wr_an": Wr_an, "Wt_nm": Wt_nm, "Wt_an": Wt_an,
            "nm_dash": np.asarray(nm, np.float32), "gate_dash": np.asarray(gate, np.float32), "grad_out": g}


def reference(x_dash, x_rear, x_right, Wd_nm, Wd_an, Wr_nm, Wr_an, Wt_nm, Wt_an, nm_dash, gate_dash, grad_out):
    dv = np.repeat(f64(grad_out)[:, :NJ], NV, axis=1)[:, :F] / NV
    dz = f64(gate_dash) * dv
    dg = np.sum(dv * f64(nm_dash), axis=1, keepdims=True)
    dx = mxq(dz, 1, "e5m2") @ mxq(f64(Wd_nm), 1, "e4m3").T
    dx = dx + dg * np.mean(f64(Wd_an), axis=1)[None, :]
    dw = mxq(f64(x_dash), 0, "e4m3").T @ mxq(dz, 0, "e5m2")
    return dx, dw

@@ -1,0 +1,306 @@
+from contextlib import ExitStack
+
+import concourse.mybir as mybir
+from concourse.masks import make_identity
+
+B, DIN, F = 1024, 1024, 1024
+NV = 3
+NJ = (F + NV - 1) // NV
+
+FLOPS = 2 * B * F * DIN + 2 * DIN * B * F
+BYTES = 3 * 2 * DIN * F + 4 * B * F + 4 * B + 2 * B * NJ + 2 * 4 * B * DIN
+
+F32 = mybir.dt.float32
+BF16 = mybir.dt.bfloat16
+U32 = mybir.dt.uint32
+U8 = mybir.dt.uint8
+E4M3 = mybir.dt.float8_e4m3fn_x4
+E5M2 = mybir.dt.float8_e5m2_x4
+ALU = mybir.AluOpType
+ACT = mybir.ActivationFunctionType
+
+P = 128
+PACK = 4
+K_PASS = P * PACK
+PASSES = 2
+N = 512
+TILES = 8
+HALF = 4
+WIDE = NJ * NV
+G_ROW = 352
+DZ_ROW = 1056
+F32_ROW = 1032
+NM_ROWS = 2
+CHUNK = 64
+
+
+def tile_fusion_r3d_pa_v_kernel(
+    tc, x_dash, x_rear, x_right, Wd_nm, Wd_an, Wr_nm, Wr_an, Wt_nm, Wt_an, nm_dash, gate_dash, grad_out, out_0, out_1
+):
+    nc = tc.nc
+
+    with ExitStack() as ctx:
+        keep = ctx.enter_context(tc.tile_pool(name="keep", bufs=1))
+        dz_pool = ctx.enter_context(tc.tile_pool(name="dz", bufs=4))
+        psum = ctx.enter_context(tc.psum_pool(name="psum", bufs=1))
+        ctx.enter_context(tc.manual_schedule())
+
+        def sbuf(name, shape, dtype):
+            return keep.tile(shape, dtype, name=name, align_bytes=64)
+
+        def bank(k):
+            return psum.tile([P, N], F32, name="bank%d" % k)
+
+        def triple(ap):
+            return ap.unsqueeze(2).to_broadcast([P, NJ, NV])
+
+        def by_three(ap):
+            return ap.rearrange("p (w e) -> p w e", e=NV)
+
+        gate = sbuf("gate", [P, PASSES, PACK], F32)
+        gate3 = sbuf("gate3", [P, TILES], F32)
+        grad = [sbuf("grad%d" % g, [P, PACK, G_ROW], BF16) for g in range(PASSES)]
+        x_raw = [sbuf("x_raw%d" % g, [P, PACK, DIN], BF16) for g in range(PASSES)]
+        w_raw = [sbuf("w_raw%d" % h, [P, HALF, F], BF16) for h in range(2)]
+        wan = sbuf("wan", [P, TILES, F], BF16)
+        nm = [sbuf("nm%d" % q, [P, NM_ROWS, F32_ROW], F32) for q in range(TILES // NM_ROWS)]
+        r_rows = [sbuf("r_rows%d" % g, [P, PACK, G_ROW], BF16) for g in range(PASSES)]
+        r_in = [sbuf("r_in%d" % g, [P, N * PACK], BF16) for g in range(PASSES)]
+        r_codes = [sbuf("r_codes%d" % g, [P, N], U32) for g in range(PASSES)]
+        r_scales = [sbuf("r_scales%d" % g, [P, N], U8) for g in range(PASSES)]
+        x_in = [sbuf("x_in%d" % k, [P, N * PACK], BF16) for k in range(2 * PASSES)]
+        x_codes = [sbuf("x_codes%d" % k, [P, N], U32) for k in range(2 * PASSES)]
+        x_scales = [sbuf("x_scales%d" % k, [P, N], U8) for k in range(2 * PASSES)]
+        z_in = [sbuf("z_in%d" % g, [P, PACK * F], BF16) for g in range(PASSES)]
+        z_codes = [sbuf("z_codes%d" % g, [P, F], U32) for g in range(PASSES)]
+        z_scales = [sbuf("z_scales%d" % g, [P, F], U8) for g in range(PASSES)]
+        w_in = [sbuf("w_in%d" % h, [P, HALF * F], BF16) for h in range(2)]
+        w_codes = [sbuf("w_codes%d" % h, [P, F], U32) for h in range(2)]
+        w_scales = [sbuf("w_scales%d" % h, [P, F], U8) for h in range(2)]
+        dw = [sbuf("dw%d" % t, [P, F32_ROW], F32) for t in range(TILES)]
+        dg = sbuf("dg", [P, TILES], F32)
+        m_sum = sbuf("m_sum", [P, TILES], F32)
+        m_row = [sbuf("m_row%d" % h, [P, N], F32) for h in range(2)]
+        ident = sbuf("ident", [P, P], F32)
+        ident_bf = sbuf("ident_bf", [P, P], BF16)
+
+        tokens = "(g p j) w -> g p j w"
+        grad_v = grad_out.rearrange(tokens, p=P, j=PACK)
+        x_v = x_dash.rearrange(tokens, p=P, j=PACK)
+        nm_v = nm_dash.rearrange(tokens, p=P, j=PACK)
+        dx_v = out_0.rearrange(tokens, p=P, j=PACK)
+        w_v = Wd_nm.rearrange("(r p) c -> p r c", p=P)
+        wan_v = Wd_an.rearrange("(r p) c -> p r c", p=P)
+
+        def load_nm(q):
+            g, j0 = divmod(q * NM_ROWS, PACK)
+            nc.sync.dma_start(out=nm[q][:, :, :F], in_=nm_v[g, :, j0 : j0 + NM_ROWS, :])
+
+        nc.sync.dma_start(out=gate[:], in_=gate_dash.rearrange("(g p j) o -> p g (j o)", p=P, j=PACK))
+        for g in range(PASSES):
+            nc.sync.dma_start(out=grad[g][:, :, :NJ], in_=grad_v[g, :, :, :NJ])
+        for g in range(PASSES):
+            nc.sync.dma_start(out=x_raw[g][:], in_=x_v[g])
+        for h in range(2):
+            nc.sync.dma_start(out=w_raw[h][:], in_=w_v[:, h * HALF : (h + 1) * HALF, :])
+        load_nm(0)
+        for h in range(2):
+            nc.sync.dma_start(out=wan[:, h * HALF : (h + 1) * HALF, :], in_=wan_v[:, h * HALF : (h + 1) * HALF, :])
+        for q in range(1, TILES // NM_ROWS):
+            load_nm(q)
+
+        make_identity(nc, ident[:])
+        nc.scalar.activation(out=ident_bf[:], in_=ident[:], func=ACT.Copy)
+        for g in range(PASSES):
+            nc.vector.memset(r_in[g][:, NJ * PACK :], 0.0)
+        for q in range(TILES // NM_ROWS):
+            nc.vector.memset(nm[q][:, :, F:], 0.0)
+        nc.vector.tensor_scalar(
+            out=gate3[:], in0=gate[:].rearrange("p g j -> p (g j)"), scalar1=1.0 / NV, scalar2=None, op0=ALU.mult
+        )
+
+        def transpose_words(rows, k):
+            words = rows.bitcast(F32)
+            turned = bank(k)
+            for f in range(PASSES):
+                for u in range(2):
+                    at = (2 * f + u) * P
+                    nc.tensor.transpose(turned[:, at : at + P], words[:, 2 * P * f + u : 2 * P * (f + 1) : 2], ident[:])
+            return turned
+
+        def pair_up(turned, dst):
+            nc.scalar.copy(out=dst, in_=turned[:].rearrange("p (f u n) -> p f n u", f=PASSES, u=2))
+
+        def z_slot(t):
+            g, j = divmod(t, PACK)
+            return z_in[g][:].bitcast(F32).rearrange("p (j f n u) -> p j f n u", j=PACK, f=PASSES, u=2)[:, j]
+
+        def w_slot(t):
+            h, r = divmod(t, HALF)
+            return w_in[h][:].bitcast(F32).rearrange("p (f r n u) -> p r f n u", f=PASSES, r=HALF, u=2)[:, r]
+
+        def quantize(src, codes, scales, fmt):
+            nc.vector.quantize_mx(out=codes[:].bitcast(fmt), scales=scales[:], in_=src[:])
+
+        def r_round(g):
+            for j in range(PACK):
+                t = g * PACK + j
+                nc.vector.tensor_scalar(
+                    out=r_rows[g][:, j, :NJ], in0=grad[g][:, j, :NJ], scalar1=gate3[:, t : t + 1], scalar2=None, op0=ALU.mult
+                )
+
+        def r_interleave(g):
+            nc.vector.tensor_copy(
+                out=r_in[g][:, : NJ * PACK].rearrange("p (w j) -> p w j", j=PACK),
+                in_=r_rows[g][:, :, :NJ].rearrange("p j w -> p w j"),
+            )
+
+        def x_interleave(k):
+            g, h = divmod(k, 2)
+            nc.vector.tensor_copy(
+                out=x_in[k][:].rearrange("p (c i j) -> p c j i", i=4, j=PACK),
+                in_=x_raw[g][:, :, h * N : (h + 1) * N].rearrange("p j (c i) -> p c j i", i=4),
+            )
+
+        def x_quantize(k):
+            quantize(x_in[k], x_codes[k], x_scales[k], E4M3)
+
+        def nm_row(t):
+            q, j = divmod(t, NM_ROWS)
+            return nm[q][:, j, :]
+
+        def gate_grad(t):
+            g, j = divmod(t, PACK)
+            row = by_three(nm_row(t)[:, :WIDE])
+            nc.vector.scalar_tensor_tensor(
+                out=row, in0=row, scalar=1.0 / NV, in1=triple(grad[g][:, j, :NJ]),
+                op0=ALU.mult, op1=ALU.mult, accum_out=dg[:, t : t + 1],
+            )
+
+        def dw_matmul(t):
+            h, r = divmod(t, HALF)
+            acc = bank(4 + t % 3)
+            cols = slice(r * P, (r + 1) * P)
+            for g in range(PASSES):
+                nc.tensor.matmul_mx(
+                    out=acc[:],
+                    lhsT=x_codes[2 * g + h][:, cols].bitcast(E4M3), lhsT_scale=x_scales[2 * g + h][:, cols],
+                    rhs=r_codes[g][:].bitcast(E5M2), rhs_scale=r_scales[g][:],
+                    start=(g == 0), stop=(g == PASSES - 1),
+                )
+            return acc
+
+        def dw_out(t, acc):
+            nc.scalar.copy(out=by_three(dw[t][:, :WIDE]), in_=triple(acc[:, :NJ]))
+            nc.sync.dma_start(out=out_1[t * P : (t + 1) * P, :], in_=dw[t][:, :F])
+
+        dx_banks = (2, 3, 7, 0, 1)
+
+        def dx_matmul(s):
+            t, h = divmod(s, 2)
+            g, j = divmod(t, PACK)
+            acc = bank(dx_banks[s % len(dx_banks)])
+            for f in range(PASSES):
+                z_cols = slice((j * PASSES + f) * P, (j * PASSES + f + 1) * P)
+                w_cols = slice(f * N, (f + 1) * N)
+                nc.tensor.matmul_mx(
+                    out=acc[:],
+                    lhsT=z_codes[g][:, z_cols].bitcast(E5M2), lhsT_scale=z_scales[g][:, z_cols],
+                    rhs=w_codes[h][:, w_cols].bitcast(E4M3), rhs_scale=w_scales[h][:, w_cols],
+                    start=(f == 0), stop=(f == PASSES - 1),
+                )
+            return acc
+
+        def dx_out(s, acc):
+            t, h = divmod(s, 2)
+            g, j = divmod(t, PACK)
+            nc.vector.scalar_tensor_tensor(
+                out=nm_row(t)[:, h * N : (h + 1) * N], in0=m_row[h][:], scalar=dg[:, t : t + 1], in1=acc[:],
+                op0=ALU.mult, op1=ALU.add,
+            )
+            if h == 1:
+                nc.sync.dma_start(out=dx_v[g, :, j, :], in_=nm_row(t)[:, :F])
+
+        z_turned = {}
+        w_turned = {}
+        for t in range(TILES):
+            g, j = divmod(t, PACK)
+            dz = dz_pool.tile([P, DZ_ROW], BF16, name="dz", align_bytes=64)
+            nc.scalar.activation(
+                out=by_three(dz[:, :WIDE]), in_=triple(grad[g][:, j, :NJ]), func=ACT.Copy, scale=gate3[:, t : t + 1]
+            )
+            z_turned[t] = transpose_words(dz[:, :F], t % 4)
+            if t >= HALF:
+                w_turned[t - HALF] = transpose_words(w_raw[0][:, t - HALF, :], t)
+            if t >= 1:
+                pair_up(z_turned[t - 1], z_slot(t - 1))
+        pair_up(z_turned[TILES - 1], z_slot(TILES - 1))
+        for r in range(HALF):
+            w_turned[HALF + r] = transpose_words(w_raw[1][:, r, :], r)
+        for t in range(TILES):
+            pair_up(w_turned[t], w_slot(t))
+
+        r_round(0)
+        r_interleave(0)
+        r_round(1)
+        quantize(r_in[0], r_codes[0], r_scales[0], E5M2)
+        r_interleave(1)
+        x_interleave(0)
+        quantize(r_in[1], r_codes[1], r_scales[1], E5M2)
+        for k in range(1, 2 * PASSES):
+            x_interleave(k)
+            x_quantize(k - 1)
+        quantize(z_in[0], z_codes[0], z_scales[0], E5M2)
+        x_quantize(2 * PASSES - 1)
+        gate_grad(0)
+        gate_grad(1)
+        quantize(z_in[1], z_codes[1], z_scales[1], E5M2)
+        for h in range(2):
+            quantize(w_in[h], w_codes[h], w_scales[h], E4M3)
+        gate_grad(2)
+        gate_grad(3)
+
+        dw_acc = {}
+        for t in range(3):
+            dw_acc[t] = dw_matmul(t)
+        partial = bank(7)
+        chunks = F // CHUNK
+        for c in range(chunks):
+            nc.tensor.matmul(
+                out=partial[:].rearrange("p (r n) -> p r n", r=TILES), lhsT=ident_bf[:],
+                rhs=wan[:, :, c * CHUNK : (c + 1) * CHUNK], start=(c == 0), stop=(c == chunks - 1),
+            )
+        nc.vector.tensor_reduce(
+            out=m_sum[:], in_=partial[:].rearrange("p (r n) -> p r n", r=TILES), axis=mybir.AxisListType.X, op=ALU.add
+        )
+        for t in range(HALF, TILES):
+            gate_grad(t)
+        dw_out(0, dw_acc[0])
+        dw_acc[3] = dw_matmul(3)
+        spread = {}
+        for h in range(2):
+            spread[h] = bank(h)
+            for r in range(HALF):
+                t = h * HALF + r
+                nc.tensor.transpose(spread[h][:, r * P : (r + 1) * P], m_sum[:, t : t + 1].to_broadcast([P, P]), ident[:])
+        for t in range(1, 3):
+            dw_out(t, dw_acc[t])
+            dw_acc[t + 3] = dw_matmul(t + 3)
+        dx_acc = {}
+        for s in range(3):
+            dx_acc[s] = dx_matmul(s)
+        dw_out(3, dw_acc[3])
+        dw_acc[6] = dw_matmul(6)
+        for h in range(2):
+            nc.scalar.activation(out=m_row[h][:], in_=spread[h][:], func=ACT.Copy, scale=1.0 / F)
+        dw_out(4, dw_acc[4])
+        dw_acc[7] = dw_matmul(7)
+        for t in range(5, TILES):
+            dw_out(t, dw_acc[t])
+        ahead = len(dx_banks)
+        for s in range(3, ahead):
+            dx_acc[s] = dx_matmul(s)
+        for s in range(2 * TILES):
+            dx_out(s, dx_acc[s])
+            if s + ahead < 2 * TILES:
+                dx_acc[s + ahead] = dx_matmul(s + ahead)

@@ -27,9 +27,9 @@ N = 512
 TILES = 8
 HALF = 4
 WIDE = NJ * NV
-G_ROW = 352
+G_ROW = 384
 DZ_ROW = 1056
-F32_ROW = 1032
+DW_ROW = 1088
 NM_ROWS = 2
 CHUNK = 64
 
@@ -42,28 +42,32 @@ def tile_fusion_r3d_pa_v_kernel(
     with ExitStack() as ctx:
         keep = ctx.enter_context(tc.tile_pool(name="keep", bufs=1))
         dz_pool = ctx.enter_context(tc.tile_pool(name="dz", bufs=4))
+        dw_pool = ctx.enter_context(tc.tile_pool(name="dw", bufs=7))
         psum = ctx.enter_context(tc.psum_pool(name="psum", bufs=1))
         ctx.enter_context(tc.manual_schedule())
 
         def sbuf(name, shape, dtype):
             return keep.tile(shape, dtype, name=name, align_bytes=64)
 
+        def dma_tile(name, shape, dtype):
+            return keep.tile(shape, dtype, name=name, align_bytes=256)
+
         def bank(k):
             return psum.tile([P, N], F32, name="bank%d" % k)
 
         def triple(ap):
-            return ap.unsqueeze(2).to_broadcast([P, NJ, NV])
+            return ap.unsqueeze(2).to_broadcast([P, ap.shape[1], NV])
 
         def by_three(ap):
             return ap.rearrange("p (w e) -> p w e", e=NV)
 
         gate = sbuf("gate", [P, PASSES, PACK], F32)
         gate3 = sbuf("gate3", [P, TILES], F32)
-        grad = [sbuf("grad%d" % g, [P, PACK, G_ROW], BF16) for g in range(PASSES)]
-        x_raw = [sbuf("x_raw%d" % g, [P, PACK, DIN], BF16) for g in range(PASSES)]
-        w_raw = [sbuf("w_raw%d" % h, [P, HALF, F], BF16) for h in range(2)]
-        wan = sbuf("wan", [P, TILES, F], BF16)
-        nm = [sbuf("nm%d" % q, [P, NM_ROWS, F32_ROW], F32) for q in range(TILES // NM_ROWS)]
+        grad = [dma_tile("grad%d" % g, [P, PACK, G_ROW], BF16) for g in range(PASSES)]
+        x_raw = [dma_tile("x_raw%d" % g, [P, PACK, DIN], BF16) for g in range(PASSES)]
+        w_raw = [dma_tile("w_raw%d" % h, [P, HALF, F], BF16) for h in range(2)]
+        wan = dma_tile("wan", [P, TILES, F], BF16)
+        nm = [dma_tile("nm%d" % g, [P, PACK, F], F32) for g in range(PASSES)]
         r_rows = [sbuf("r_rows%d" % g, [P, PACK, G_ROW], BF16) for g in range(PASSES)]
         r_in = [sbuf("r_in%d" % g, [P, N * PACK], BF16) for g in range(PASSES)]
         r_codes = [sbuf("r_codes%d" % g, [P, N], U32) for g in range(PASSES)]
@@ -77,7 +81,8 @@ def tile_fusion_r3d_pa_v_kernel(
         w_in = [sbuf("w_in%d" % h, [P, HALF * F], BF16) for h in range(2)]
         w_codes = [sbuf("w_codes%d" % h, [P, F], U32) for h in range(2)]
         w_scales = [sbuf("w_scales%d" % h, [P, F], U8) for h in range(2)]
-        dw = [sbuf("dw%d" % t, [P, F32_ROW], F32) for t in range(TILES)]
+        dg_main = sbuf("dg_main", [P, TILES], F32)
+        dg_last = sbuf("dg_last", [P, TILES], F32)
         dg = sbuf("dg", [P, TILES], F32)
         m_sum = sbuf("m_sum", [P, TILES], F32)
         m_row = [sbuf("m_row%d" % h, [P, N], F32) for h in range(2)]
@@ -89,12 +94,12 @@ def tile_fusion_r3d_pa_v_kernel(
         x_v = x_dash.rearrange(tokens, p=P, j=PACK)
         nm_v = nm_dash.rearrange(tokens, p=P, j=PACK)
         dx_v = out_0.rearrange(tokens, p=P, j=PACK)
-        w_v = Wd_nm.rearrange("(r p) c -> p r c", p=P)
-        wan_v = Wd_an.rearrange("(r p) c -> p r c", p=P)
+        w_v = Wd_nm.rearrange("(h p r) c -> h p r c", p=P, r=HALF)
+        wan_v = Wd_an.rearrange("(h p r) c -> h p r c", p=P, r=HALF)
 
         def load_nm(q):
             g, j0 = divmod(q * NM_ROWS, PACK)
-            nc.sync.dma_start(out=nm[q][:, :, :F], in_=nm_v[g, :, j0 : j0 + NM_ROWS, :])
+            nc.sync.dma_start(out=nm[g][:, j0 : j0 + NM_ROWS, :], in_=nm_v[g, :, j0 : j0 + NM_ROWS, :])
 
         nc.sync.dma_start(out=gate[:], in_=gate_dash.rearrange("(g p j) o -> p g (j o)", p=P, j=PACK))
         for g in range(PASSES):
@@ -102,10 +107,10 @@ def tile_fusion_r3d_pa_v_kernel(
         for g in range(PASSES):
             nc.sync.dma_start(out=x_raw[g][:], in_=x_v[g])
         for h in range(2):
-            nc.sync.dma_start(out=w_raw[h][:], in_=w_v[:, h * HALF : (h + 1) * HALF, :])
+            nc.sync.dma_start(out=w_raw[h][:], in_=w_v[h])
         load_nm(0)
         for h in range(2):
-            nc.sync.dma_start(out=wan[:, h * HALF : (h + 1) * HALF, :], in_=wan_v[:, h * HALF : (h + 1) * HALF, :])
+            nc.sync.dma_start(out=wan[:, h * HALF : (h + 1) * HALF, :], in_=wan_v[h])
         for q in range(1, TILES // NM_ROWS):
             load_nm(q)
 
@@ -113,31 +118,41 @@ def tile_fusion_r3d_pa_v_kernel(
         nc.scalar.activation(out=ident_bf[:], in_=ident[:], func=ACT.Copy)
         for g in range(PASSES):
             nc.vector.memset(r_in[g][:, NJ * PACK :], 0.0)
-        for q in range(TILES // NM_ROWS):
-            nc.vector.memset(nm[q][:, :, F:], 0.0)
         nc.vector.tensor_scalar(
             out=gate3[:], in0=gate[:].rearrange("p g j -> p (g j)"), scalar1=1.0 / NV, scalar2=None, op0=ALU.mult
         )
 
-        def transpose_words(rows, k):
-            words = rows.bitcast(F32)
+        def every_second_word(rows, f, u):
+            return rows.bitcast(F32)[:, 2 * P * f + u : 2 * P * (f + 1) : 2]
+
+        def transpose_four(sources, k):
             turned = bank(k)
-            for f in range(PASSES):
-                for u in range(2):
-                    at = (2 * f + u) * P
-                    nc.tensor.transpose(turned[:, at : at + P], words[:, 2 * P * f + u : 2 * P * (f + 1) : 2], ident[:])
+            for s, src in enumerate(sources):
+                nc.tensor.transpose(turned[:, s * P : (s + 1) * P], src, ident[:])
             return turned
 
-        def pair_up(turned, dst):
-            nc.scalar.copy(out=dst, in_=turned[:].rearrange("p (f u n) -> p f n u", f=PASSES, u=2))
+        def z_transpose(dz, k):
+            return transpose_four([every_second_word(dz, f, u) for f in range(PASSES) for u in range(2)], k)
 
-        def z_slot(t):
+        def z_pair_up(t, turned):
             g, j = divmod(t, PACK)
-            return z_in[g][:].bitcast(F32).rearrange("p (j f n u) -> p j f n u", j=PACK, f=PASSES, u=2)[:, j]
+            nc.scalar.copy(
+                out=z_in[g][:].bitcast(F32).rearrange("p (j f n u) -> p j f n u", j=PACK, f=PASSES, u=2)[:, j],
+                in_=turned[:].rearrange("p (f u n) -> p f n u", f=PASSES, u=2),
+            )
 
-        def w_slot(t):
-            h, r = divmod(t, HALF)
-            return w_in[h][:].bitcast(F32).rearrange("p (f r n u) -> p r f n u", f=PASSES, r=HALF, u=2)[:, r]
+        def w_transpose(s, k):
+            h, f, pair = s // 4, s // 2 % 2, s % 2
+            return transpose_four(
+                [every_second_word(w_raw[h][:, 2 * pair + r, :], f, u) for r in range(2) for u in range(2)], k
+            )
+
+        def w_pair_up(s, turned):
+            h, f, pair = s // 4, s // 2 % 2, s % 2
+            nc.scalar.copy(
+                out=w_in[h][:].bitcast(F32).rearrange("p (f n a b) -> p f a n b", f=PASSES, a=2, b=4)[:, f, pair],
+                in_=turned[:].rearrange("p (b n) -> p n b", b=4),
+            )
 
         def quantize(src, codes, scales, fmt):
             nc.vector.quantize_mx(out=codes[:].bitcast(fmt), scales=scales[:], in_=src[:])
@@ -165,16 +180,23 @@ def tile_fusion_r3d_pa_v_kernel(
         def x_quantize(k):
             quantize(x_in[k], x_codes[k], x_scales[k], E4M3)
 
-        def nm_row(t):
-            q, j = divmod(t, NM_ROWS)
-            return nm[q][:, j, :]
-
         def gate_grad(t):
             g, j = divmod(t, PACK)
-            row = by_three(nm_row(t)[:, :WIDE])
+            full = (NJ - 1) * NV
             nc.vector.scalar_tensor_tensor(
-                out=row, in0=row, scalar=1.0 / NV, in1=triple(grad[g][:, j, :NJ]),
-                op0=ALU.mult, op1=ALU.mult, accum_out=dg[:, t : t + 1],
+                out=by_three(x_in[j][:].bitcast(F32)[:, :full]), in0=by_three(nm[g][:, j, :full]), scalar=1.0 / NV,
+                in1=triple(grad[g][:, j, : NJ - 1]), op0=ALU.mult, op1=ALU.mult, accum_out=dg_main[:, t : t + 1],
+            )
+
+        def gate_grad_last(g):
+            nc.vector.tensor_tensor(
+                out=dg_last[:, g * PACK : (g + 1) * PACK], in0=nm[g][:, :, F - 1], in1=grad[g][:, :, NJ - 1], op=ALU.mult
+            )
+
+        def gate_grad_join(g):
+            cols = slice(g * PACK, (g + 1) * PACK)
+            nc.vector.scalar_tensor_tensor(
+                out=dg[:, cols], in0=dg_last[:, cols], scalar=1.0 / NV, in1=dg_main[:, cols], op0=ALU.mult, op1=ALU.add
             )
 
         def dw_matmul(t):
@@ -191,8 +213,9 @@ def tile_fusion_r3d_pa_v_kernel(
             return acc
 
         def dw_out(t, acc):
-            nc.scalar.copy(out=by_three(dw[t][:, :WIDE]), in_=triple(acc[:, :NJ]))
-            nc.sync.dma_start(out=out_1[t * P : (t + 1) * P, :], in_=dw[t][:, :F])
+            dw = dw_pool.tile([P, DW_ROW], F32, name="dw", align_bytes=256)
+            nc.scalar.copy(out=by_three(dw[:, :WIDE]), in_=triple(acc[:, :NJ]))
+            nc.sync.dma_start(out=out_1[t * P : (t + 1) * P, :], in_=dw[:, :F])
 
         dx_banks = (2, 3, 7, 0, 1)
 
@@ -215,11 +238,12 @@ def tile_fusion_r3d_pa_v_kernel(
             t, h = divmod(s, 2)
             g, j = divmod(t, PACK)
             nc.vector.scalar_tensor_tensor(
-                out=nm_row(t)[:, h * N : (h + 1) * N], in0=m_row[h][:], scalar=dg[:, t : t + 1], in1=acc[:],
+                out=nm[g][:, j, h * N : (h + 1) * N], in0=m_row[h][:], scalar=dg[:, t : t + 1], in1=acc[:],
                 op0=ALU.mult, op1=ALU.add,
             )
-            if h == 1:
-                nc.sync.dma_start(out=dx_v[g, :, j, :], in_=nm_row(t)[:, :F])
+            rows = 1 if t >= TILES - NM_ROWS else NM_ROWS
+            if h == 1 and (j + 1) % rows == 0:
+                nc.sync.dma_start(out=dx_v[g, :, j + 1 - rows : j + 1, :], in_=nm[g][:, j + 1 - rows : j + 1, :])
 
         z_turned = {}
         w_turned = {}
@@ -229,16 +253,16 @@ def tile_fusion_r3d_pa_v_kernel(
             nc.scalar.activation(
                 out=by_three(dz[:, :WIDE]), in_=triple(grad[g][:, j, :NJ]), func=ACT.Copy, scale=gate3[:, t : t + 1]
             )
-            z_turned[t] = transpose_words(dz[:, :F], t % 4)
+            z_turned[t] = z_transpose(dz[:, :F], t % 4)
             if t >= HALF:
-                w_turned[t - HALF] = transpose_words(w_raw[0][:, t - HALF, :], t)
+                w_turned[t - HALF] = w_transpose(t - HALF, t)
             if t >= 1:
-                pair_up(z_turned[t - 1], z_slot(t - 1))
-        pair_up(z_turned[TILES - 1], z_slot(TILES - 1))
+                z_pair_up(t - 1, z_turned[t - 1])
+        z_pair_up(TILES - 1, z_turned[TILES - 1])
         for r in range(HALF):
-            w_turned[HALF + r] = transpose_words(w_raw[1][:, r, :], r)
+            w_turned[HALF + r] = w_transpose(HALF + r, r)
         for t in range(TILES):
-            pair_up(w_turned[t], w_slot(t))
+            w_pair_up(t, w_turned[t])
 
         r_round(0)
         r_interleave(0)
@@ -259,6 +283,7 @@ def tile_fusion_r3d_pa_v_kernel(
             quantize(w_in[h], w_codes[h], w_scales[h], E4M3)
         gate_grad(2)
         gate_grad(3)
+        gate_grad_last(0)
 
         dw_acc = {}
         for t in range(3):
@@ -273,8 +298,10 @@ def tile_fusion_r3d_pa_v_kernel(
         nc.vector.tensor_reduce(
             out=m_sum[:], in_=partial[:].rearrange("p (r n) -> p r n", r=TILES), axis=mybir.AxisListType.X, op=ALU.add
         )
+        gate_grad_join(0)
         for t in range(HALF, TILES):
             gate_grad(t)
+        gate_grad_last(1)
         dw_out(0, dw_acc[0])
         dw_acc[3] = dw_matmul(3)
         spread = {}
@@ -292,7 +319,10 @@ def tile_fusion_r3d_pa_v_kernel(
         dw_out(3, dw_acc[3])
         dw_acc[6] = dw_matmul(6)
         for h in range(2):
-            nc.scalar.activation(out=m_row[h][:], in_=spread[h][:], func=ACT.Copy, scale=1.0 / F)
+            nc.scalar.activation(
+                out=m_row[h][:].rearrange("p (n r) -> p n r", r=HALF),
+                in_=spread[h][:].rearrange("p (r n) -> p n r", r=HALF), func=ACT.Copy, scale=1.0 / F,
+            )
         dw_out(4, dw_acc[4])
         dw_acc[7] = dw_matmul(7)
         for t in range(5, TILES):
@@ -302,5 +332,7 @@ def tile_fusion_r3d_pa_v_kernel(
             dx_acc[s] = dx_matmul(s)
         for s in range(2 * TILES):
             dx_out(s, dx_acc[s])
+            if s == 0:
+                gate_grad_join(1)
             if s + ahead < 2 * TILES:
                 dx_acc[s + ahead] = dx_matmul(s + ahead)

@@ -66,7 +66,7 @@ def tile_fusion_r3d_pa_v_kernel(
         grad = [dma_tile("grad%d" % g, [P, PACK, G_ROW], BF16) for g in range(PASSES)]
         x_raw = [dma_tile("x_raw%d" % g, [P, PACK, DIN], BF16) for g in range(PASSES)]
         w_raw = [dma_tile("w_raw%d" % h, [P, HALF, F], BF16) for h in range(2)]
-        wan = dma_tile("wan", [P, TILES, F], BF16)
+        wan = [dma_tile("wan%d" % h, [P, HALF, F], BF16) for h in range(2)]
         nm = [dma_tile("nm%d" % g, [P, PACK, F], F32) for g in range(PASSES)]
         r_rows = [sbuf("r_rows%d" % g, [P, PACK, G_ROW], BF16) for g in range(PASSES)]
         r_in = [sbuf("r_in%d" % g, [P, N * PACK], BF16) for g in range(PASSES)]
@@ -104,14 +104,14 @@ def tile_fusion_r3d_pa_v_kernel(
         nc.sync.dma_start(out=gate[:], in_=gate_dash.rearrange("(g p j) o -> p g (j o)", p=P, j=PACK))
         for g in range(PASSES):
             nc.sync.dma_start(out=grad[g][:, :, :NJ], in_=grad_v[g, :, :, :NJ])
-        for g in range(PASSES):
-            nc.sync.dma_start(out=x_raw[g][:], in_=x_v[g])
-        for h in range(2):
-            nc.sync.dma_start(out=w_raw[h][:], in_=w_v[h])
+        nc.sync.dma_start(out=x_raw[0][:], in_=x_v[0])
+        nc.sync.dma_start(out=w_raw[0][:], in_=w_v[0])
+        nc.sync.dma_start(out=x_raw[1][:], in_=x_v[1])
+        nc.sync.dma_start(out=wan[0][:], in_=wan_v[0])
+        nc.sync.dma_start(out=w_raw[1][:], in_=w_v[1])
         load_nm(0)
-        for h in range(2):
-            nc.sync.dma_start(out=wan[:, h * HALF : (h + 1) * HALF, :], in_=wan_v[h])
-        for q in range(1, TILES // NM_ROWS):
+        nc.sync.dma_start(out=wan[1][:], in_=wan_v[1])
+        for q in range(1, 4):
             load_nm(q)
 
         make_identity(nc, ident[:])
@@ -193,15 +193,15 @@ def tile_fusion_r3d_pa_v_kernel(
                 out=dg_last[:, g * PACK : (g + 1) * PACK], in0=nm[g][:, :, F - 1], in1=grad[g][:, :, NJ - 1], op=ALU.mult
             )
 
-        def gate_grad_join(g):
-            cols = slice(g * PACK, (g + 1) * PACK)
+        def gate_grad_join(t0, t1):
+            cols = slice(t0, t1)
             nc.vector.scalar_tensor_tensor(
                 out=dg[:, cols], in0=dg_last[:, cols], scalar=1.0 / NV, in1=dg_main[:, cols], op0=ALU.mult, op1=ALU.add
             )
 
-        def dw_matmul(t):
+        def dw_matmul(t, k):
             h, r = divmod(t, HALF)
-            acc = bank(4 + t % 3)
+            acc = bank(k)
             cols = slice(r * P, (r + 1) * P)
             for g in range(PASSES):
                 nc.tensor.matmul_mx(
@@ -215,9 +215,12 @@ def tile_fusion_r3d_pa_v_kernel(
         def dw_out(t, acc):
             dw = dw_pool.tile([P, DW_ROW], F32, name="dw", align_bytes=256)
             nc.scalar.copy(out=by_three(dw[:, :WIDE]), in_=triple(acc[:, :NJ]))
+            return dw
+
+        def dw_store(t, dw):
             nc.sync.dma_start(out=out_1[t * P : (t + 1) * P, :], in_=dw[:, :F])
 
-        dx_banks = (2, 3, 7, 0, 1)
+        dx_banks = (4, 7, 2, 3)
 
         def dx_matmul(s):
             t, h = divmod(s, 2)
@@ -241,29 +244,75 @@ def tile_fusion_r3d_pa_v_kernel(
                 out=nm[g][:, j, h * N : (h + 1) * N], in0=m_row[h][:], scalar=dg[:, t : t + 1], in1=acc[:],
                 op0=ALU.mult, op1=ALU.add,
             )
-            rows = 1 if t >= TILES - NM_ROWS else NM_ROWS
+            rows = 1 if t >= HALF else NM_ROWS
             if h == 1 and (j + 1) % rows == 0:
                 nc.sync.dma_start(out=dx_v[g, :, j + 1 - rows : j + 1, :], in_=nm[g][:, j + 1 - rows : j + 1, :])
 
+        chunks = F // CHUNK
+        partial = bank(7)
+
+        def mean_matmuls(h, c0, c1):
+            cols = slice(h * HALF * CHUNK, (h + 1) * HALF * CHUNK)
+            for c in range(c0, c1):
+                nc.tensor.matmul(
+                    out=partial[:, cols].rearrange("p (r n) -> p r n", r=HALF), lhsT=ident_bf[:],
+                    rhs=wan[h][:, :, c * CHUNK : (c + 1) * CHUNK], start=(c == 0), stop=(c == chunks - 1),
+                )
+
         z_turned = {}
         w_turned = {}
-        for t in range(TILES):
+        dw_acc = {}
+        dx_acc = {}
+        spread = {}
+        ahead = len(dx_banks)
+
+        def dz_make(t):
             g, j = divmod(t, PACK)
             dz = dz_pool.tile([P, DZ_ROW], BF16, name="dz", align_bytes=64)
             nc.scalar.activation(
                 out=by_three(dz[:, :WIDE]), in_=triple(grad[g][:, j, :NJ]), func=ACT.Copy, scale=gate3[:, t : t + 1]
             )
-            z_turned[t] = z_transpose(dz[:, :F], t % 4)
-            if t >= HALF:
-                w_turned[t - HALF] = w_transpose(t - HALF, t)
+            z_turned[t] = z_transpose(dz[:, :F], t % 2)
+            if t in (1, 2, 3, 4):
+                keep_warm()
+
+        def keep_warm():
+            spare = bank(5)
+            nc.tensor.matmul(
+                out=spare[:, : 2 * P].rearrange("p (a n) -> p a n", a=2), lhsT=ident[:],
+                rhs=ident[:].unsqueeze(1).to_broadcast([P, 2, P]), start=True, stop=True,
+            )
+
+        def w_turn(s):
+            w_turned[s] = w_transpose(s, 2 + s % 3)
+
+        def mean_reduce():
+            nc.vector.tensor_reduce(
+                out=m_sum[:], in_=partial[:].rearrange("p (r n) -> p r n", r=TILES), axis=mybir.AxisListType.X, op=ALU.add
+            )
+
+        def mean_spread(h, k):
+            spread[h] = bank(k)
+            for r in range(HALF):
+                t = h * HALF + r
+                nc.tensor.transpose(spread[h][:, r * P : (r + 1) * P], m_sum[:, t : t + 1].to_broadcast([P, P]), ident[:])
+
+        def mean_row(h):
+            nc.scalar.activation(
+                out=m_row[h][:].rearrange("p (n r) -> p n r", r=HALF),
+                in_=spread[h][:].rearrange("p (r n) -> p n r", r=HALF), func=ACT.Copy, scale=1.0 / F,
+            )
+
+        for t in range(4):
+            dz_make(t)
             if t >= 1:
                 z_pair_up(t - 1, z_turned[t - 1])
-        z_pair_up(TILES - 1, z_turned[TILES - 1])
-        for r in range(HALF):
-            w_turned[HALF + r] = w_transpose(HALF + r, r)
-        for t in range(TILES):
-            w_pair_up(t, w_turned[t])
-
+        w_turn(0)
+        w_turn(1)
+        dz_make(4)
+        w_turn(2)
+        z_pair_up(3, z_turned[3])
+        w_pair_up(0, w_turned[0])
         r_round(0)
         r_interleave(0)
         r_round(1)
@@ -276,63 +325,75 @@ def tile_fusion_r3d_pa_v_kernel(
             x_quantize(k - 1)
         quantize(z_in[0], z_codes[0], z_scales[0], E5M2)
         x_quantize(2 * PASSES - 1)
+        dz_make(5)
+        w_turn(3)
+        mean_matmuls(0, 0, 8)
+        z_pair_up(4, z_turned[4])
+        w_pair_up(1, w_turned[1])
+        w_pair_up(2, w_turned[2])
+        dz_make(6)
+        w_turn(4)
+        mean_matmuls(0, 8, 12)
+        w_turn(5)
+        z_pair_up(5, z_turned[5])
+        w_pair_up(3, w_turned[3])
+        dz_make(7)
+        mean_matmuls(0, 12, 16)
+        w_turn(6)
+        z_pair_up(6, z_turned[6])
+        w_pair_up(4, w_turned[4])
+        w_turn(7)
+        dw_acc[0] = dw_matmul(0, 5)
+        dw_acc[1] = dw_matmul(1, 6)
+        z_pair_up(7, z_turned[7])
+        for s in (5, 6, 7):
+            w_pair_up(s, w_turned[s])
+        mean_matmuls(1, 0, chunks)
+        dw_acc[2] = dw_matmul(2, 0)
+        dw_acc[3] = dw_matmul(3, 1)
+        quantize(w_in[0], w_codes[0], w_scales[0], E4M3)
         gate_grad(0)
         gate_grad(1)
         quantize(z_in[1], z_codes[1], z_scales[1], E5M2)
-        for h in range(2):
-            quantize(w_in[h], w_codes[h], w_scales[h], E4M3)
         gate_grad(2)
+        quantize(w_in[1], w_codes[1], w_scales[1], E4M3)
+        mean_reduce()
         gate_grad(3)
         gate_grad_last(0)
-
-        dw_acc = {}
-        for t in range(3):
-            dw_acc[t] = dw_matmul(t)
-        partial = bank(7)
-        chunks = F // CHUNK
-        for c in range(chunks):
-            nc.tensor.matmul(
-                out=partial[:].rearrange("p (r n) -> p r n", r=TILES), lhsT=ident_bf[:],
-                rhs=wan[:, :, c * CHUNK : (c + 1) * CHUNK], start=(c == 0), stop=(c == chunks - 1),
-            )
-        nc.vector.tensor_reduce(
-            out=m_sum[:], in_=partial[:].rearrange("p (r n) -> p r n", r=TILES), axis=mybir.AxisListType.X, op=ALU.add
-        )
-        gate_grad_join(0)
-        for t in range(HALF, TILES):
-            gate_grad(t)
-        gate_grad_last(1)
-        dw_out(0, dw_acc[0])
-        dw_acc[3] = dw_matmul(3)
-        spread = {}
-        for h in range(2):
-            spread[h] = bank(h)
-            for r in range(HALF):
-                t = h * HALF + r
-                nc.tensor.transpose(spread[h][:, r * P : (r + 1) * P], m_sum[:, t : t + 1].to_broadcast([P, P]), ident[:])
-        for t in range(1, 3):
-            dw_out(t, dw_acc[t])
-            dw_acc[t + 3] = dw_matmul(t + 3)
-        dx_acc = {}
-        for s in range(3):
-            dx_acc[s] = dx_matmul(s)
-        dw_out(3, dw_acc[3])
-        dw_acc[6] = dw_matmul(6)
-        for h in range(2):
-            nc.scalar.activation(
-                out=m_row[h][:].rearrange("p (n r) -> p n r", r=HALF),
-                in_=spread[h][:].rearrange("p (r n) -> p n r", r=HALF), func=ACT.Copy, scale=1.0 / F,
-            )
-        dw_out(4, dw_acc[4])
-        dw_acc[7] = dw_matmul(7)
-        for t in range(5, TILES):
-            dw_out(t, dw_acc[t])
-        ahead = len(dx_banks)
-        for s in range(3, ahead):
-            dx_acc[s] = dx_matmul(s)
+        gate_grad(4)
+        gate_grad_join(0, HALF)
+        gate_grad(5)
+        dw_store(0, dw_out(0, dw_acc[0]))
+        dw_acc[4] = dw_matmul(4, 5)
+        dw_store(1, dw_out(1, dw_acc[1]))
+        dw_acc[5] = dw_matmul(5, 6)
+        mean_spread(0, 2)
+        mean_spread(1, 3)
+        dx_acc[0] = dx_matmul(0)
+        dx_acc[1] = dx_matmul(1)
+        dw_store(2, dw_out(2, dw_acc[2]))
+        dw_acc[6] = dw_matmul(6, 0)
+        dw_store(3, dw_out(3, dw_acc[3]))
+        dw_acc[7] = dw_matmul(7, 1)
+        mean_row(0)
+        mean_row(1)
+        dx_acc[2] = dx_matmul(2)
+        dx_acc[3] = dx_matmul(3)
+        for t in (4, 5, 6):
+            dw_store(t, dw_out(t, dw_acc[t]))
+        dw_last = dw_out(7, dw_acc[7])
         for s in range(2 * TILES):
             dx_out(s, dx_acc[s])
-            if s == 0:
-                gate_grad_join(1)
+            if s == 3:
+                dw_store(7, dw_last)
+                gate_grad_last(1)
+            if s == 5:
+                gate_grad_join(4, 6)
+            if s == 7:
+                gate_grad(6)
+            if s == 9:
+                gate_grad(7)
+            if s == 10:
+                gate_grad_join(6, 8)
             if s + ahead < 2 * TILES:
                 dx_acc[s + ahead] = dx_matmul(s + ahead)

@@ -273,15 +273,6 @@ def tile_fusion_r3d_pa_v_kernel(
                 out=by_three(dz[:, :WIDE]), in_=triple(grad[g][:, j, :NJ]), func=ACT.Copy, scale=gate3[:, t : t + 1]
             )
             z_turned[t] = z_transpose(dz[:, :F], t % 2)
-            if t in (1, 2, 3, 4):
-                keep_warm()
-
-        def keep_warm():
-            spare = bank(5)
-            nc.tensor.matmul(
-                out=spare[:, : 2 * P].rearrange("p (a n) -> p a n", a=2), lhsT=ident[:],
-                rhs=ident[:].unsqueeze(1).to_broadcast([P, 2, P]), start=True, stop=True,
-            )
 
         def w_turn(s):
             w_turned[s] = w_transpose(s, 2 + s % 3)

from contextlib import ExitStack

import concourse.mybir as mybir
from concourse.masks import make_identity

B, DIN, F = 1024, 1024, 1024
NV = 3
NJ = (F + NV - 1) // NV

FLOPS = 2 * B * F * DIN + 2 * DIN * B * F
BYTES = 3 * 2 * DIN * F + 4 * B * F + 4 * B + 2 * B * NJ + 2 * 4 * B * DIN

F32 = mybir.dt.float32
BF16 = mybir.dt.bfloat16
U32 = mybir.dt.uint32
U8 = mybir.dt.uint8
E4M3 = mybir.dt.float8_e4m3fn_x4
E5M2 = mybir.dt.float8_e5m2_x4
ALU = mybir.AluOpType
ACT = mybir.ActivationFunctionType

P = 128
PACK = 4
K_PASS = P * PACK
PASSES = 2
N = 512
TILES = 8
HALF = 4
WIDE = NJ * NV
G_ROW = 384
DZ_ROW = 1056
DW_ROW = 1088
NM_ROWS = 2
CHUNK = 64


def tile_fusion_r3d_pa_v_kernel(
    tc, x_dash, x_rear, x_right, Wd_nm, Wd_an, Wr_nm, Wr_an, Wt_nm, Wt_an, nm_dash, gate_dash, grad_out, out_0, out_1
):
    nc = tc.nc

    with ExitStack() as ctx:
        keep = ctx.enter_context(tc.tile_pool(name="keep", bufs=1))
        dz_pool = ctx.enter_context(tc.tile_pool(name="dz", bufs=4))
        dw_pool = ctx.enter_context(tc.tile_pool(name="dw", bufs=7))
        psum = ctx.enter_context(tc.psum_pool(name="psum", bufs=1))
        ctx.enter_context(tc.manual_schedule())

        def sbuf(name, shape, dtype):
            return keep.tile(shape, dtype, name=name, align_bytes=64)

        def dma_tile(name, shape, dtype):
            return keep.tile(shape, dtype, name=name, align_bytes=256)

        def bank(k):
            return psum.tile([P, N], F32, name="bank%d" % k)

        def triple(ap):
            return ap.unsqueeze(2).to_broadcast([P, ap.shape[1], NV])

        def by_three(ap):
            return ap.rearrange("p (w e) -> p w e", e=NV)

        gate = sbuf("gate", [P, PASSES, PACK], F32)
        gate3 = sbuf("gate3", [P, TILES], F32)
        grad = [dma_tile("grad%d" % g, [P, PACK, G_ROW], BF16) for g in range(PASSES)]
        x_raw = [dma_tile("x_raw%d" % g, [P, PACK, DIN], BF16) for g in range(PASSES)]
        w_raw = [dma_tile("w_raw%d" % h, [P, HALF, F], BF16) for h in range(2)]
        wan = [dma_tile("wan%d" % h, [P, HALF, F], BF16) for h in range(2)]
        nm = [dma_tile("nm%d" % g, [P, PACK, F], F32) for g in range(PASSES)]
        r_rows = [sbuf("r_rows%d" % g, [P, PACK, G_ROW], BF16) for g in range(PASSES)]
        r_in = [sbuf("r_in%d" % g, [P, N * PACK], BF16) for g in range(PASSES)]
        r_codes = [sbuf("r_codes%d" % g, [P, N], U32) for g in range(PASSES)]
        r_scales = [sbuf("r_scales%d" % g, [P, N], U8) for g in range(PASSES)]
        x_in = [sbuf("x_in%d" % k, [P, N * PACK], BF16) for k in range(2 * PASSES)]
        x_codes = [sbuf("x_codes%d" % k, [P, N], U32) for k in range(2 * PASSES)]
        x_scales = [sbuf("x_scales%d" % k, [P, N], U8) for k in range(2 * PASSES)]
        z_in = [sbuf("z_in%d" % g, [P, PACK * F], BF16) for g in range(PASSES)]
        z_codes = [sbuf("z_codes%d" % g, [P, F], U32) for g in range(PASSES)]
        z_scales = [sbuf("z_scales%d" % g, [P, F], U8) for g in range(PASSES)]
        w_in = [sbuf("w_in%d" % h, [P, HALF * F], BF16) for h in range(2)]
        w_codes = [sbuf("w_codes%d" % h, [P, F], U32) for h in range(2)]
        w_scales = [sbuf("w_scales%d" % h, [P, F], U8) for h in range(2)]
        dg_main = sbuf("dg_main", [P, TILES], F32)
        dg_last = sbuf("dg_last", [P, TILES], F32)
        dg = sbuf("dg", [P, TILES], F32)
        m_sum = sbuf("m_sum", [P, TILES], F32)
        m_row = [sbuf("m_row%d" % h, [P, N], F32) for h in range(2)]
        ident = sbuf("ident", [P, P], F32)
        ident_bf = sbuf("ident_bf", [P, P], BF16)

        tokens = "(g p j) w -> g p j w"
        grad_v = grad_out.rearrange(tokens, p=P, j=PACK)
        x_v = x_dash.rearrange(tokens, p=P, j=PACK)
        nm_v = nm_dash.rearrange(tokens, p=P, j=PACK)
        dx_v = out_0.rearrange(tokens, p=P, j=PACK)
        w_v = Wd_nm.rearrange("(h p r) c -> h p r c", p=P, r=HALF)
        wan_v = Wd_an.rearrange("(h p r) c -> h p r c", p=P, r=HALF)

        def load_nm(q):
            g, j0 = divmod(q * NM_ROWS, PACK)
            nc.sync.dma_start(out=nm[g][:, j0 : j0 + NM_ROWS, :], in_=nm_v[g, :, j0 : j0 + NM_ROWS, :])

        nc.sync.dma_start(out=gate[:], in_=gate_dash.rearrange("(g p j) o -> p g (j o)", p=P, j=PACK))
        for g in range(PASSES):
            nc.sync.dma_start(out=grad[g][:, :, :NJ], in_=grad_v[g, :, :, :NJ])
        nc.sync.dma_start(out=x_raw[0][:], in_=x_v[0])
        nc.sync.dma_start(out=w_raw[0][:], in_=w_v[0])
        nc.sync.dma_start(out=x_raw[1][:], in_=x_v[1])
        nc.sync.dma_start(out=wan[0][:], in_=wan_v[0])
        nc.sync.dma_start(out=w_raw[1][:], in_=w_v[1])
        load_nm(0)
        nc.sync.dma_start(out=wan[1][:], in_=wan_v[1])
        for q in range(1, 4):
            load_nm(q)

        make_identity(nc, ident[:])
        nc.scalar.activation(out=ident_bf[:], in_=ident[:], func=ACT.Copy)
        for g in range(PASSES):
            nc.vector.memset(r_in[g][:, NJ * PACK :], 0.0)
        nc.vector.tensor_scalar(
            out=gate3[:], in0=gate[:].rearrange("p g j -> p (g j)"), scalar1=1.0 / NV, scalar2=None, op0=ALU.mult
        )

        def every_second_word(rows, f, u):
            return rows.bitcast(F32)[:, 2 * P * f + u : 2 * P * (f + 1) : 2]

        def transpose_four(sources, k):
            turned = bank(k)
            for s, src in enumerate(sources):
                nc.tensor.transpose(turned[:, s * P : (s + 1) * P], src, ident[:])
            return turned

        def z_transpose(dz, k):
            return transpose_four([every_second_word(dz, f, u) for f in range(PASSES) for u in range(2)], k)

        def z_pair_up(t, turned):
            g, j = divmod(t, PACK)
            nc.scalar.copy(
                out=z_in[g][:].bitcast(F32).rearrange("p (j f n u) -> p j f n u", j=PACK, f=PASSES, u=2)[:, j],
                in_=turned[:].rearrange("p (f u n) -> p f n u", f=PASSES, u=2),
            )

        def w_transpose(s, k):
            h, f, pair = s // 4, s // 2 % 2, s % 2
            return transpose_four(
                [every_second_word(w_raw[h][:, 2 * pair + r, :], f, u) for r in range(2) for u in range(2)], k
            )

        def w_pair_up(s, turned):
            h, f, pair = s // 4, s // 2 % 2, s % 2
            nc.scalar.copy(
                out=w_in[h][:].bitcast(F32).rearrange("p (f n a b) -> p f a n b", f=PASSES, a=2, b=4)[:, f, pair],
                in_=turned[:].rearrange("p (b n) -> p n b", b=4),
            )

        def quantize(src, codes, scales, fmt):
            nc.vector.quantize_mx(out=codes[:].bitcast(fmt), scales=scales[:], in_=src[:])

        def r_round(g):
            for j in range(PACK):
                t = g * PACK + j
                nc.vector.tensor_scalar(
                    out=r_rows[g][:, j, :NJ], in0=grad[g][:, j, :NJ], scalar1=gate3[:, t : t + 1], scalar2=None, op0=ALU.mult
                )

        def r_interleave(g):
            nc.vector.tensor_copy(
                out=r_in[g][:, : NJ * PACK].rearrange("p (w j) -> p w j", j=PACK),
                in_=r_rows[g][:, :, :NJ].rearrange("p j w -> p w j"),
            )

        def x_interleave(k):
            g, h = divmod(k, 2)
            nc.vector.tensor_copy(
                out=x_in[k][:].rearrange("p (c i j) -> p c j i", i=4, j=PACK),
                in_=x_raw[g][:, :, h * N : (h + 1) * N].rearrange("p j (c i) -> p c j i", i=4),
            )

        def x_quantize(k):
            quantize(x_in[k], x_codes[k], x_scales[k], E4M3)

        def gate_grad(t):
            g, j = divmod(t, PACK)
            full = (NJ - 1) * NV
            nc.vector.scalar_tensor_tensor(
                out=by_three(x_in[j][:].bitcast(F32)[:, :full]), in0=by_three(nm[g][:, j, :full]), scalar=1.0 / NV,
                in1=triple(grad[g][:, j, : NJ - 1]), op0=ALU.mult, op1=ALU.mult, accum_out=dg_main[:, t : t + 1],
            )

        def gate_grad_last(g):
            nc.vector.tensor_tensor(
                out=dg_last[:, g * PACK : (g + 1) * PACK], in0=nm[g][:, :, F - 1], in1=grad[g][:, :, NJ - 1], op=ALU.mult
            )

        def gate_grad_join(t0, t1):
            cols = slice(t0, t1)
            nc.vector.scalar_tensor_tensor(
                out=dg[:, cols], in0=dg_last[:, cols], scalar=1.0 / NV, in1=dg_main[:, cols], op0=ALU.mult, op1=ALU.add
            )

        def dw_matmul(t, k):
            h, r = divmod(t, HALF)
            acc = bank(k)
            cols = slice(r * P, (r + 1) * P)
            for g in range(PASSES):
                nc.tensor.matmul_mx(
                    out=acc[:],
                    lhsT=x_codes[2 * g + h][:, cols].bitcast(E4M3), lhsT_scale=x_scales[2 * g + h][:, cols],
                    rhs=r_codes[g][:].bitcast(E5M2), rhs_scale=r_scales[g][:],
                    start=(g == 0), stop=(g == PASSES - 1),
                )
            return acc

        def dw_out(t, acc):
            dw = dw_pool.tile([P, DW_ROW], F32, name="dw", align_bytes=256)
            nc.scalar.copy(out=by_three(dw[:, :WIDE]), in_=triple(acc[:, :NJ]))
            return dw

        def dw_store(t, dw):
            nc.sync.dma_start(out=out_1[t * P : (t + 1) * P, :], in_=dw[:, :F])

        dx_banks = (4, 7, 2, 3)

        def dx_matmul(s):
            t, h = divmod(s, 2)
            g, j = divmod(t, PACK)
            acc = bank(dx_banks[s % len(dx_banks)])
            for f in range(PASSES):
                z_cols = slice((j * PASSES + f) * P, (j * PASSES + f + 1) * P)
                w_cols = slice(f * N, (f + 1) * N)
                nc.tensor.matmul_mx(
                    out=acc[:],
                    lhsT=z_codes[g][:, z_cols].bitcast(E5M2), lhsT_scale=z_scales[g][:, z_cols],
                    rhs=w_codes[h][:, w_cols].bitcast(E4M3), rhs_scale=w_scales[h][:, w_cols],
                    start=(f == 0), stop=(f == PASSES - 1),
                )
            return acc

        def dx_out(s, acc):
            t, h = divmod(s, 2)
            g, j = divmod(t, PACK)
            nc.vector.scalar_tensor_tensor(
                out=nm[g][:, j, h * N : (h + 1) * N], in0=m_row[h][:], scalar=dg[:, t : t + 1], in1=acc[:],
                op0=ALU.mult, op1=ALU.add,
            )
            rows = 1 if t >= HALF else NM_ROWS
            if h == 1 and (j + 1) % rows == 0:
                nc.sync.dma_start(out=dx_v[g, :, j + 1 - rows : j + 1, :], in_=nm[g][:, j + 1 - rows : j + 1, :])

        chunks = F // CHUNK
        partial = bank(7)

        def mean_matmuls(h, c0, c1):
            cols = slice(h * HALF * CHUNK, (h + 1) * HALF * CHUNK)
            for c in range(c0, c1):
                nc.tensor.matmul(
                    out=partial[:, cols].rearrange("p (r n) -> p r n", r=HALF), lhsT=ident_bf[:],
                    rhs=wan[h][:, :, c * CHUNK : (c + 1) * CHUNK], start=(c == 0), stop=(c == chunks - 1),
                )

        z_turned = {}
        w_turned = {}
        dw_acc = {}
        dx_acc = {}
        spread = {}
        ahead = len(dx_banks)

        def dz_make(t):
            g, j = divmod(t, PACK)
            dz = dz_pool.tile([P, DZ_ROW], BF16, name="dz", align_bytes=64)
            nc.scalar.activation(
                out=by_three(dz[:, :WIDE]), in_=triple(grad[g][:, j, :NJ]), func=ACT.Copy, scale=gate3[:, t : t + 1]
            )
            z_turned[t] = z_transpose(dz[:, :F], t % 2)

        def w_turn(s):
            w_turned[s] = w_transpose(s, 2 + s % 3)

        def mean_reduce():
            nc.vector.tensor_reduce(
                out=m_sum[:], in_=partial[:].rearrange("p (r n) -> p r n", r=TILES), axis=mybir.AxisListType.X, op=ALU.add
            )

        def mean_spread(h, k):
            spread[h] = bank(k)
            for r in range(HALF):
                t = h * HALF + r
                nc.tensor.transpose(spread[h][:, r * P : (r + 1) * P], m_sum[:, t : t + 1].to_broadcast([P, P]), ident[:])

        def mean_row(h):
            nc.scalar.activation(
                out=m_row[h][:].rearrange("p (n r) -> p n r", r=HALF),
                in_=spread[h][:].rearrange("p (r n) -> p n r", r=HALF), func=ACT.Copy, scale=1.0 / F,
            )

        for t in range(4):
            dz_make(t)
            if t >= 1:
                z_pair_up(t - 1, z_turned[t - 1])
        w_turn(0)
        w_turn(1)
        dz_make(4)
        w_turn(2)
        z_pair_up(3, z_turned[3])
        w_pair_up(0, w_turned[0])
        r_round(0)
        r_interleave(0)
        r_round(1)
        quantize(r_in[0], r_codes[0], r_scales[0], E5M2)
        r_interleave(1)
        x_interleave(0)
        quantize(r_in[1], r_codes[1], r_scales[1], E5M2)
        for k in range(1, 2 * PASSES):
            x_interleave(k)
            x_quantize(k - 1)
        quantize(z_in[0], z_codes[0], z_scales[0], E5M2)
        x_quantize(2 * PASSES - 1)
        dz_make(5)
        w_turn(3)
        mean_matmuls(0, 0, 8)
        z_pair_up(4, z_turned[4])
        w_pair_up(1, w_turned[1])
        w_pair_up(2, w_turned[2])
        dz_make(6)
        w_turn(4)
        mean_matmuls(0, 8, 12)
        w_turn(5)
        z_pair_up(5, z_turned[5])
        w_pair_up(3, w_turned[3])
        dz_make(7)
        mean_matmuls(0, 12, 16)
        w_turn(6)
        z_pair_up(6, z_turned[6])
        w_pair_up(4, w_turned[4])
        w_turn(7)
        dw_acc[0] = dw_matmul(0, 5)
        dw_acc[1] = dw_matmul(1, 6)
        z_pair_up(7, z_turned[7])
        for s in (5, 6, 7):
            w_pair_up(s, w_turned[s])
        mean_matmuls(1, 0, chunks)
        dw_acc[2] = dw_matmul(2, 0)
        dw_acc[3] = dw_matmul(3, 1)
        quantize(w_in[0], w_codes[0], w_scales[0], E4M3)
        gate_grad(0)
        gate_grad(1)
        quantize(z_in[1], z_codes[1], z_scales[1], E5M2)
        gate_grad(2)
        quantize(w_in[1], w_codes[1], w_scales[1], E4M3)
        mean_reduce()
        gate_grad(3)
        gate_grad_last(0)
        gate_grad(4)
        gate_grad_join(0, HALF)
        gate_grad(5)
        dw_store(0, dw_out(0, dw_acc[0]))
        dw_acc[4] = dw_matmul(4, 5)
        dw_store(1, dw_out(1, dw_acc[1]))
        dw_acc[5] = dw_matmul(5, 6)
        mean_spread(0, 2)
        mean_spread(1, 3)
        dx_acc[0] = dx_matmul(0)
        dx_acc[1] = dx_matmul(1)
        dw_store(2, dw_out(2, dw_acc[2]))
        dw_acc[6] = dw_matmul(6, 0)
        dw_store(3, dw_out(3, dw_acc[3]))
        dw_acc[7] = dw_matmul(7, 1)
        mean_row(0)
        mean_row(1)
        dx_acc[2] = dx_matmul(2)
        dx_acc[3] = dx_matmul(3)
        for t in (4, 5, 6):
            dw_store(t, dw_out(t, dw_acc[t]))
        dw_last = dw_out(7, dw_acc[7])
        for s in range(2 * TILES):
            dx_out(s, dx_acc[s])
            if s == 3:
                dw_store(7, dw_last)
                gate_grad_last(1)
            if s == 5:
                gate_grad_join(4, 6)
            if s == 7:
                gate_grad(6)
            if s == 9:
                gate_grad(7)
            if s == 10:
                gate_grad_join(6, 8)
            if s + ahead < 2 * TILES:
                dx_acc[s + ahead] = dx_matmul(s + ahead)
